import numpy as np
import ml_dtypes


def mxq(x, axis, fmt="e4m3"):
    dtype, down = {"e4m3": (ml_dtypes.float8_e4m3fn, 7), "e5m2": (ml_dtypes.float8_e5m2, 14)}[fmt]
    v = np.moveaxis(np.asarray(x, np.float32).astype(ml_dtypes.bfloat16).astype(np.float64), axis, -1)
    blocks = v.reshape(v.shape[:-1] + (-1, 32))
    amax = np.abs(blocks).max(-1, keepdims=True)
    byte = np.maximum(np.where(amax > 0, np.frexp(amax)[1] - 1 + 127, 0) - down, 1)
    scale = np.exp2(byte - 127.0)
    codes = (blocks / scale).astype(np.float32).astype(dtype).astype(np.float64)
    return np.moveaxis((codes * scale).reshape(v.shape), -1, axis)


WIDE = False


def mx_kscale(k):
    if not WIDE:
        return np.ones(k)
    levels = np.array([10, -10, 5, -5, 0])
    if k % 512:
        return np.exp2(np.random.permutation(np.resize(levels, k // 32))).repeat(32)
    a = np.empty((k // 512, 16))
    for p in range(k // 512):
        a[p, :8] = np.random.permutation(np.resize(levels, 8))
        for g in range(8):
            far = levels[np.abs(levels - a[p, g]) >= 10]
            a[p, g + 8] = far[np.random.randint(len(far))]
    return np.exp2(a.ravel()).repeat(32)


BF16 = ml_dtypes.bfloat16


def bf(x):
    return np.asarray(x, np.float32).astype(BF16)


def f64(x):
    return np.asarray(x).astype(np.float64)


N_A, N_P, D = 2048, 2048, 512
TEMPERATURE = 0.07
SIG = 3.5
SA = np.sqrt(SIG * TEMPERATURE / np.sqrt(D))
SP = SA * np.sqrt(SIG ** 2 - 2.0 * np.log(N_P / N_A)) / SIG


def logsumexp(v):
    m = v.max(axis=1, keepdims=True)
    return m[:, 0] + np.log(np.exp(v - m).sum(axis=1))


def setup_inputs():
    s = mx_kscale(D)
    c = np.mean(s ** 4) ** -0.25
    return {"anchor": bf(np.random.standard_normal((N_A, D)) * SA * s * c),
            "pos": bf(np.random.standard_normal((N_P, D)) * SP / (s * c))}


def reference(anchor, pos):
    aq = mxq(f64(anchor), 1, "e4m3")
    sim_pos = (aq @ mxq(f64(pos), 1, "e4m3").T) / TEMPERATURE
    sim_neg = (aq @ aq.T) / TEMPERATURE
    sim_neg = np.where(np.eye(aq.shape[0], dtype=bool), -np.inf, sim_neg)
    numerator = logsumexp(sim_pos)
    denominator = np.logaddexp(numerator, logsumexp(sim_neg))
    return numerator - denominator

@@ -1,0 +1,261 @@
+from contextlib import ExitStack
+
+import concourse.mybir as mybir
+from concourse.masks import make_identity
+
+F32 = mybir.dt.float32
+BF16 = mybir.dt.bfloat16
+U32 = mybir.dt.uint32
+U8 = mybir.dt.uint8
+FP8X4 = mybir.dt.float8_e4m3fn_x4
+ALU = mybir.AluOpType
+ACT = mybir.ActivationFunctionType
+AXIS_X = mybir.AxisListType.X
+
+P = 128
+PACK = 4
+ROWS = 2048
+FEATURES = 512
+ROW_TILES = ROWS // P
+BANK = 512
+PSUM_BANKS = 8
+CHUNK_TILES = BANK // P
+CHUNKS = ROW_TILES // CHUNK_TILES
+HALF_TILES = CHUNK_TILES // 2
+WORD_HALVES = 2
+POS, NEG = 0, 1
+PARTS = 2 * CHUNKS
+TEMPERATURE = 0.07
+MASK_ROOT = 2.0**50
+FAR_BELOW = -1.0e30
+
+CHUNK_ORDER = [("anchor", c) for c in range(CHUNKS)] + [("pos", c) for c in range(CHUNKS)]
+STEPS_PER_CHUNK = 3
+HEAD_STEPS = 2 * STEPS_PER_CHUNK + 2
+LEAD = 2
+
+FLOPS = 2 * 2 * ROWS * ROWS * FEATURES
+
+
+def banks_opened_by(stage):
+    name, chunk = CHUNK_ORDER[stage]
+    if name == "pos":
+        return [(r, POS, chunk) for r in range(ROW_TILES)]
+    return [
+        (r, NEG, c)
+        for r in range((chunk + 1) * CHUNK_TILES)
+        for c in range(chunk + 1)
+        if r // CHUNK_TILES == chunk or c == chunk
+    ]
+
+
+def tile_crossgenderinfonceloss_pa_kernel(tc, anchor, pos, out):
+    nc = tc.nc
+    with ExitStack() as stack:
+        stack.enter_context(tc.manual_schedule())
+        keep = stack.enter_context(tc.tile_pool(name="keep", bufs=1))
+        stage_pool = stack.enter_context(tc.tile_pool(name="stage", bufs=3))
+        unread = stack.enter_context(tc.tile_pool(name="unread", bufs=4))
+        psum = stack.enter_context(tc.psum_pool(name="psum", bufs=PSUM_BANKS))
+
+        sources = {"anchor": anchor, "pos": pos}
+        raw = {}
+        for name in ("anchor", "pos"):
+            raw[name] = keep.tile([P, ROW_TILES, FEATURES], BF16, name="raw_" + name)
+        for name, chunk in CHUNK_ORDER:
+            for half in range(2):
+                first = chunk * CHUNK_TILES + half * HALF_TILES
+                nc.sync.dma_start(
+                    out=raw[name][:, first : first + HALF_TILES, :],
+                    in_=sources[name].rearrange("(p r) k -> p r k", r=ROW_TILES)[
+                        :, first : first + HALF_TILES, :
+                    ],
+                )
+
+        identity = keep.tile([P, P], F32)
+        make_identity(nc, identity[:])
+        zero = keep.tile([P, 1], F32)
+        nc.vector.memset(zero[:], 0.0)
+        one = keep.tile([P, 1], F32)
+        nc.scalar.activation(out=one[:], in_=zero[:], func=ACT.Exp)
+        zero_again = keep.tile([P, 1], F32)
+
+        mask_values = keep.tile([P, 2, P, PACK], BF16, align_bytes=64)
+        spread_identity = identity[:].unsqueeze(2).to_broadcast([P, P, PACK])
+        nc.vector.tensor_scalar(
+            out=mask_values[:, 0], in0=spread_identity, scalar1=MASK_ROOT, scalar2=None, op0=ALU.mult
+        )
+        nc.vector.tensor_scalar(
+            out=mask_values[:, 1], in0=spread_identity, scalar1=-MASK_ROOT, scalar2=None, op0=ALU.mult
+        )
+        mask_codes = keep.tile([P, 2 * P], U32, align_bytes=64)
+        mask_scales = keep.tile([P, 2 * P], U8, align_bytes=64)
+        nc.vector.quantize_mx(
+            out=mask_codes[:].bitcast(FP8X4),
+            scales=mask_scales[:],
+            in_=mask_values[:].rearrange("p s m j -> p (s m j)"),
+        )
+
+        codes = {}
+        scales = {}
+        for name in ("anchor", "pos"):
+            codes[name] = keep.tile([P, ROWS], U32, name="codes_" + name, align_bytes=64)
+            scales[name] = keep.tile([P, ROWS], U8, name="scales_" + name, align_bytes=64)
+
+        top = keep.tile([P, ROW_TILES * PARTS], F32)
+        shift = keep.tile([P, ROW_TILES * PARTS], F32)
+        total = keep.tile([P, ROW_TILES * PARTS], F32)
+        weight = keep.tile([P, 2, ROW_TILES, PARTS], F32)
+        nc.vector.memset(weight[:], FAR_BELOW)
+
+        grouped = {}
+
+        def flip_half(name, chunk, half):
+            if half == 0:
+                grouped[name, chunk] = stage_pool.tile(
+                    [P, BANK, PACK], BF16, name="grouped", align_bytes=64
+                )
+            words = raw[name][:].bitcast(F32)
+            flipped = psum.tile([P, HALF_TILES, WORD_HALVES, P], F32, tag="bank")
+            for t in range(HALF_TILES):
+                r = chunk * CHUNK_TILES + half * HALF_TILES + t
+                for u in range(WORD_HALVES):
+                    nc.tensor.transpose(
+                        flipped[:, t, u, :], words[:, r, u : WORD_HALVES * P : WORD_HALVES], identity[:]
+                    )
+            rows = slice(half * HALF_TILES * P, (half + 1) * HALF_TILES * P)
+            target = grouped[name, chunk][:].bitcast(F32)[:, rows, :]
+            target = target.rearrange("p (t r) u -> p t r u", t=HALF_TILES)
+            source = flipped[:].rearrange("p t u r -> p t r u")
+            if name == "anchor":
+                nc.scalar.copy(out=target, in_=source)
+            else:
+                nc.vector.tensor_copy(out=target, in_=source)
+
+        def quantise(name, chunk):
+            cols = slice(chunk * BANK, (chunk + 1) * BANK)
+            nc.vector.quantize_mx(
+                out=codes[name][:, cols].bitcast(FP8X4),
+                scales=scales[name][:, cols],
+                in_=grouped[name, chunk][:].rearrange("p w j -> p (w j)"),
+            )
+
+        def steps_of(name, chunk):
+            return [
+                lambda: flip_half(name, chunk, 0),
+                lambda: flip_half(name, chunk, 1),
+                lambda: quantise(name, chunk),
+            ]
+
+        def product(acc, r, name, cols, start, stop):
+            rows = slice(r * P, (r + 1) * P)
+            nc.tensor.matmul_mx(
+                out=acc,
+                lhsT=codes["anchor"][:, rows].bitcast(FP8X4),
+                lhsT_scale=scales["anchor"][:, rows],
+                rhs=codes[name][:, cols].bitcast(FP8X4),
+                rhs_scale=scales[name][:, cols],
+                start=start,
+                stop=stop,
+            )
+
+        def open_bank(r, x, chunk):
+            acc = psum.tile([P, BANK], F32, tag="bank")
+            if x == NEG and chunk == r // CHUNK_TILES:
+                for t in range(CHUNK_TILES):
+                    other = chunk * CHUNK_TILES + t
+                    part = acc[:, t * P : (t + 1) * P]
+                    product(part, r, "anchor", slice(other * P, (other + 1) * P), True, other != r)
+                    if other == r:
+                        nc.tensor.matmul_mx(
+                            out=part,
+                            lhsT=mask_codes[:, 0:P].bitcast(FP8X4),
+                            lhsT_scale=mask_scales[:, 0:P],
+                            rhs=mask_codes[:, P : 2 * P].bitcast(FP8X4),
+                            rhs_scale=mask_scales[:, P : 2 * P],
+                            start=False,
+                            stop=True,
+                        )
+            else:
+                name = "pos" if x == POS else "anchor"
+                product(acc[:], r, name, slice(chunk * BANK, (chunk + 1) * BANK), True, True)
+            col = slice(r * PARTS + x * CHUNKS + chunk, r * PARTS + x * CHUNKS + chunk + 1)
+            nc.vector.tensor_reduce(out=top[:, col], in_=acc[:], axis=AXIS_X, op=ALU.max)
+            nc.gpsimd.tensor_scalar(
+                out=shift[:, col],
+                in0=top[:, col],
+                scalar1=-1.0 / TEMPERATURE,
+                scalar2=0.0,
+                op0=ALU.mult,
+                op1=ALU.add,
+            )
+            return acc, col
+
+        def close_bank(acc, col):
+            exps = unread.tile([P, BANK], BF16)
+            nc.scalar.activation(
+                out=exps[:],
+                in_=acc[:],
+                func=ACT.Exp,
+                bias=shift[:, col],
+                scale=1.0 / TEMPERATURE,
+                accum_out=total[:, col],
+            )
+
+        steps = []
+        for name, chunk in CHUNK_ORDER:
+            steps.extend(steps_of(name, chunk))
+        for step in steps[:HEAD_STEPS]:
+            step()
+        taken = HEAD_STEPS
+        still_open = None
+        for stage in range(len(CHUNK_ORDER)):
+            banks = banks_opened_by(stage)
+            due = min(len(steps), (stage + 2) * STEPS_PER_CHUNK)
+            every = (len(banks) - LEAD) // max(1, due - taken)
+            for n, (r, x, chunk) in enumerate(banks):
+                newest = open_bank(r, x, chunk)
+                if still_open is not None:
+                    close_bank(*still_open)
+                still_open = newest
+                if taken < due and (n + 1) % every == 0:
+                    steps[taken]()
+                    taken += 1
+
+        shift_r = shift[:].rearrange("p (r b) -> p r b", b=PARTS)
+        total_r = total[:].rearrange("p (r b) -> p r b", b=PARTS)
+        low = keep.tile([P, 2, ROW_TILES], F32)
+        nc.vector.tensor_reduce(out=low[:, 0, :], in_=shift_r[:, :, 0:CHUNKS], axis=AXIS_X, op=ALU.min)
+        nc.vector.tensor_reduce(out=low[:, 1, :], in_=shift_r, axis=AXIS_X, op=ALU.min)
+        nc.vector.tensor_tensor(
+            out=weight[:, 0, :, 0:CHUNKS],
+            in0=low[:, 0, :].unsqueeze(2).to_broadcast([P, ROW_TILES, CHUNKS]),
+            in1=shift_r[:, :, 0:CHUNKS],
+            op=ALU.subtract,
+        )
+        nc.vector.tensor_tensor(
+            out=weight[:, 1],
+            in0=low[:, 1, :].unsqueeze(2).to_broadcast([P, ROW_TILES, PARTS]),
+            in1=shift_r,
+            op=ALU.subtract,
+        )
+        gap = keep.tile([P, ROW_TILES], F32)
+        nc.vector.tensor_tensor(out=gap[:], in0=low[:, 1, :], in1=low[:, 0, :], op=ALU.subtract)
+        nc.scalar.activation(out=weight[:], in_=weight[:], func=ACT.Exp)
+        close_bank(*still_open)
+        nc.scalar.activation(out=zero_again[:], in_=one[:], func=ACT.Ln)
+        nc.vector.tensor_tensor(
+            out=weight[:],
+            in0=weight[:],
+            in1=total_r.unsqueeze(1).to_broadcast([P, 2, ROW_TILES, PARTS]),
+            op=ALU.mult,
+        )
+        sums = keep.tile([P, 2, ROW_TILES], F32)
+        nc.vector.tensor_reduce(out=sums[:], in_=weight[:], axis=AXIS_X, op=ALU.add)
+        ratio = keep.tile([P, ROW_TILES], F32)
+        nc.vector.reciprocal(out=ratio[:], in_=sums[:, 1, :])
+        nc.vector.tensor_tensor(out=ratio[:], in0=ratio[:], in1=sums[:, 0, :], op=ALU.mult)
+        result = keep.tile([P, ROW_TILES], F32)
+        nc.scalar.activation(out=result[:], in_=ratio[:], func=ACT.Ln)
+        nc.vector.tensor_tensor(out=result[:], in0=result[:], in1=gap[:], op=ALU.add)
+        nc.sync.dma_start(out=out.rearrange("(p r) -> p r", r=ROW_TILES), in_=result[:])

@@ -30,9 +30,30 @@ MASK_ROOT = 2.0**50
 FAR_BELOW = -1.0e30
 
 CHUNK_ORDER = [("anchor", c) for c in range(CHUNKS)] + [("pos", c) for c in range(CHUNKS)]
-STEPS_PER_CHUNK = 3
-HEAD_STEPS = 2 * STEPS_PER_CHUNK + 2
-LEAD = 2
+
+
+SCALAR_COPIES = [(0, 0), (1, 0), (1, 1), (2, 0), (2, 1), (3, 0), (5, 0), (6, 0)]
+PREPARATION = {
+    0: [(2, 0)],
+    1: [(1,)],
+    2: [(2, 1)],
+    8: [(2,)],
+    12: [(3, 0)],
+    18: [(3, 1)],
+    24: [(3,)],
+    40: [(4, 0)],
+    49: [(4, 1)],
+    50: [(4,)],
+    58: [(5, 0)],
+    67: [(5, 1)],
+    68: [(5,)],
+    76: [(6, 0)],
+    85: [(6, 1)],
+    86: [(6,)],
+    94: [(7, 0)],
+    103: [(7, 1)],
+    104: [(7,)],
+}
 
 FLOPS = 2 * 2 * ROWS * ROWS * FEATURES
 
@@ -62,15 +83,14 @@ def tile_crossgenderinfonceloss_pa_kernel(tc, anchor, pos, out):
         raw = {}
         for name in ("anchor", "pos"):
             raw[name] = keep.tile([P, ROW_TILES, FEATURES], BF16, name="raw_" + name)
-        for name, chunk in CHUNK_ORDER:
-            for half in range(2):
-                first = chunk * CHUNK_TILES + half * HALF_TILES
-                nc.sync.dma_start(
-                    out=raw[name][:, first : first + HALF_TILES, :],
-                    in_=sources[name].rearrange("(p r) k -> p r k", r=ROW_TILES)[
-                        :, first : first + HALF_TILES, :
-                    ],
-                )
+        loads = [(name, chunk * CHUNK_TILES, HALF_TILES) for name, chunk in CHUNK_ORDER]
+        loads = [(name, first + half * tiles, tiles) for name, first, tiles in loads for half in range(2)]
+        loads = [("anchor", 0, 1), ("anchor", 1, 1)] + loads[1:]
+        for name, first, tiles in loads:
+            nc.sync.dma_start(
+                out=raw[name][:, first : first + tiles, :],
+                in_=sources[name].rearrange("(p r) k -> p r k", r=ROW_TILES)[:, first : first + tiles, :],
+            )
 
         identity = keep.tile([P, P], F32)
         make_identity(nc, identity[:])
@@ -110,7 +130,8 @@ def tile_crossgenderinfonceloss_pa_kernel(tc, anchor, pos, out):
 
         grouped = {}
 
-        def flip_half(name, chunk, half):
+        def flip_half(place, half):
+            name, chunk = CHUNK_ORDER[place]
             if half == 0:
                 grouped[name, chunk] = stage_pool.tile(
                     [P, BANK, PACK], BF16, name="grouped", align_bytes=64
@@ -127,25 +148,19 @@ def tile_crossgenderinfonceloss_pa_kernel(tc, anchor, pos, out):
             target = grouped[name, chunk][:].bitcast(F32)[:, rows, :]
             target = target.rearrange("p (t r) u -> p t r u", t=HALF_TILES)
             source = flipped[:].rearrange("p t u r -> p t r u")
-            if name == "anchor":
+            if (place, half) in SCALAR_COPIES:
                 nc.scalar.copy(out=target, in_=source)
             else:
                 nc.vector.tensor_copy(out=target, in_=source)
 
-        def quantise(name, chunk):
+        def quantise(place):
+            name, chunk = CHUNK_ORDER[place]
             cols = slice(chunk * BANK, (chunk + 1) * BANK)
             nc.vector.quantize_mx(
                 out=codes[name][:, cols].bitcast(FP8X4),
                 scales=scales[name][:, cols],
                 in_=grouped[name, chunk][:].rearrange("p w j -> p (w j)"),
             )
-
-        def steps_of(name, chunk):
-            return [
-                lambda: flip_half(name, chunk, 0),
-                lambda: flip_half(name, chunk, 1),
-                lambda: quantise(name, chunk),
-            ]
 
         def product(acc, r, name, cols, start, stop):
             rows = slice(r * P, (r + 1) * P)
@@ -202,25 +217,25 @@ def tile_crossgenderinfonceloss_pa_kernel(tc, anchor, pos, out):
                 accum_out=total[:, col],
             )
 
-        steps = []
-        for name, chunk in CHUNK_ORDER:
-            steps.extend(steps_of(name, chunk))
-        for step in steps[:HEAD_STEPS]:
-            step()
-        taken = HEAD_STEPS
+        flip_half(0, 0)
+        flip_half(0, 1)
+        quantise(0)
+        flip_half(1, 0)
+        flip_half(1, 1)
         still_open = None
-        for stage in range(len(CHUNK_ORDER)):
-            banks = banks_opened_by(stage)
-            due = min(len(steps), (stage + 2) * STEPS_PER_CHUNK)
-            every = (len(banks) - LEAD) // max(1, due - taken)
-            for n, (r, x, chunk) in enumerate(banks):
-                newest = open_bank(r, x, chunk)
-                if still_open is not None:
-                    close_bank(*still_open)
-                still_open = newest
-                if taken < due and (n + 1) % every == 0:
-                    steps[taken]()
-                    taken += 1
+        banks = []
+        for place in range(len(CHUNK_ORDER)):
+            banks.extend(banks_opened_by(place))
+        for n, (r, x, chunk) in enumerate(banks):
+            newest = open_bank(r, x, chunk)
+            if still_open is not None:
+                close_bank(*still_open)
+            still_open = newest
+            for step in PREPARATION.get(n, []):
+                if len(step) == 1:
+                    quantise(*step)
+                else:
+                    flip_half(*step)
 
         shift_r = shift[:].rearrange("p (r b) -> p r b", b=PARTS)
         total_r = total[:].rearrange("p (r b) -> p r b", b=PARTS)

@@ -32,7 +32,7 @@ FAR_BELOW = -1.0e30
 CHUNK_ORDER = [("anchor", c) for c in range(CHUNKS)] + [("pos", c) for c in range(CHUNKS)]
 
 
-SCALAR_COPIES = [(0, 0), (1, 0), (1, 1), (2, 0), (2, 1), (3, 0), (5, 0), (6, 0)]
+SCALAR_COPIES = [(0, 0), (1, 0), (1, 1), (2, 0), (2, 1), (3, 0), (4, 0), (5, 0), (6, 0), (7, 0)]
 PREPARATION = {
     0: [(2, 0)],
     1: [(1,)],

@@ -32,28 +32,12 @@ FAR_BELOW = -1.0e30
 CHUNK_ORDER = [("anchor", c) for c in range(CHUNKS)] + [("pos", c) for c in range(CHUNKS)]
 
 
-SCALAR_COPIES = [(0, 0), (1, 0), (1, 1), (2, 0), (2, 1), (3, 0), (4, 0), (5, 0), (6, 0), (7, 0)]
-PREPARATION = {
-    0: [(2, 0)],
-    1: [(1,)],
-    2: [(2, 1)],
-    8: [(2,)],
-    12: [(3, 0)],
-    18: [(3, 1)],
-    24: [(3,)],
-    40: [(4, 0)],
-    49: [(4, 1)],
-    50: [(4,)],
-    58: [(5, 0)],
-    67: [(5, 1)],
-    68: [(5,)],
-    76: [(6, 0)],
-    85: [(6, 1)],
-    86: [(6,)],
-    94: [(7, 0)],
-    103: [(7, 1)],
-    104: [(7,)],
-}
+STEP_BANKS = 6
+EARLY_STEPS = [(2, 0), (1,), (2, 1)]
+LATER_STEPS = [(2,)] + [step for k in range(3, 2 * CHUNKS) for step in ((k, 0), (k, 1), (k,))]
+PREPARATION = dict(
+    list(enumerate(EARLY_STEPS)) + [(STEP_BANKS * (i + 1), step) for i, step in enumerate(LATER_STEPS)]
+)
 
 FLOPS = 2 * 2 * ROWS * ROWS * FEATURES
 
@@ -148,7 +132,7 @@ def tile_crossgenderinfonceloss_pa_kernel(tc, anchor, pos, out):
             target = grouped[name, chunk][:].bitcast(F32)[:, rows, :]
             target = target.rearrange("p (t r) u -> p t r u", t=HALF_TILES)
             source = flipped[:].rearrange("p t u r -> p t r u")
-            if (place, half) in SCALAR_COPIES:
+            if half == 0 or place in (1, 2):
                 nc.scalar.copy(out=target, in_=source)
             else:
                 nc.vector.tensor_copy(out=target, in_=source)
@@ -231,11 +215,11 @@ def tile_crossgenderinfonceloss_pa_kernel(tc, anchor, pos, out):
             if still_open is not None:
                 close_bank(*still_open)
             still_open = newest
-            for step in PREPARATION.get(n, []):
-                if len(step) == 1:
-                    quantise(*step)
-                else:
-                    flip_half(*step)
+            step = PREPARATION.get(n, ())
+            if len(step) == 2:
+                flip_half(*step)
+            elif len(step) == 1:
+                quantise(*step)
 
         shift_r = shift[:].rearrange("p (r b) -> p r b", b=PARTS)
         total_r = total[:].rearrange("p (r b) -> p r b", b=PARTS)

@@ -33,11 +33,15 @@ CHUNK_ORDER = [("anchor", c) for c in range(CHUNKS)] + [("pos", c) for c in rang
 
 
 STEP_BANKS = 6
-EARLY_STEPS = [(2, 0), (1,), (2, 1)]
-LATER_STEPS = [(2,)] + [step for k in range(3, 2 * CHUNKS) for step in ((k, 0), (k, 1), (k,))]
+EARLY_STEPS = [(2, 1), (1,)]
+LATER_STEPS = [(2,)] + [step for k in range(3, 2 * CHUNKS - 1) for step in ((k, 0), (k, 1), (k,))]
 PREPARATION = dict(
-    list(enumerate(EARLY_STEPS)) + [(STEP_BANKS * (i + 1), step) for i, step in enumerate(LATER_STEPS)]
+    list(enumerate(EARLY_STEPS))
+    + [(STEP_BANKS * (i + 1), step) for i, step in enumerate(LATER_STEPS)]
+    + [(106, (2 * CHUNKS - 1,))]
 )
+
+WARM_UP = 7
 
 FLOPS = 2 * 2 * ROWS * ROWS * FEATURES
 
@@ -70,11 +74,31 @@ def tile_crossgenderinfonceloss_pa_kernel(tc, anchor, pos, out):
         loads = [(name, chunk * CHUNK_TILES, HALF_TILES) for name, chunk in CHUNK_ORDER]
         loads = [(name, first + half * tiles, tiles) for name, first, tiles in loads for half in range(2)]
         loads = [("anchor", 0, 1), ("anchor", 1, 1)] + loads[1:]
-        for name, first, tiles in loads:
+        for name, first, tiles in loads[: len(loads) - 2]:
             nc.sync.dma_start(
                 out=raw[name][:, first : first + tiles, :],
                 in_=sources[name].rearrange("(p r) k -> p r k", r=ROW_TILES)[:, first : first + tiles, :],
             )
+
+        gathered = keep.tile([P, BANK, PACK], BF16, align_bytes=64)
+
+        def gather(queue, t):
+            name, chunk = CHUNK_ORDER[-1]
+            queue.dma_start(
+                out=gathered[:, t * P : (t + 1) * P, :],
+                in_=sources[name].rearrange("(w r) (q j) -> q r w j", r=ROW_TILES, j=PACK)[
+                    :, chunk * CHUNK_TILES + t
+                ],
+            )
+
+        for t in range(CHUNK_TILES - 1):
+            gather(nc.sync, t)
+
+        nothing = keep.tile([P, 2 * P], BF16)
+        nc.vector.memset(nothing[:], 0.0)
+        nowhere = psum.tile([P, BANK], F32, tag="bank")
+        for i in range(WARM_UP):
+            nc.tensor.matmul(nowhere[:, 0 : 2 * P], lhsT=nothing[:, 0:P], rhs=nothing[:], start=True, stop=True)
 
         identity = keep.tile([P, P], F32)
         make_identity(nc, identity[:])
@@ -112,7 +136,7 @@ def tile_crossgenderinfonceloss_pa_kernel(tc, anchor, pos, out):
         weight = keep.tile([P, 2, ROW_TILES, PARTS], F32)
         nc.vector.memset(weight[:], FAR_BELOW)
 
-        grouped = {}
+        grouped = {CHUNK_ORDER[-1]: gathered}
 
         def flip_half(place, half):
             name, chunk = CHUNK_ORDER[place]
@@ -206,6 +230,7 @@ def tile_crossgenderinfonceloss_pa_kernel(tc, anchor, pos, out):
         quantise(0)
         flip_half(1, 0)
         flip_half(1, 1)
+        flip_half(2, 0)
         still_open = None
         banks = []
         for place in range(len(CHUNK_ORDER)):
@@ -215,6 +240,8 @@ def tile_crossgenderinfonceloss_pa_kernel(tc, anchor, pos, out):
             if still_open is not None:
                 close_bank(*still_open)
             still_open = newest
+            if n == 8:
+                gather(nc.scalar, CHUNK_TILES - 1)
             step = PREPARATION.get(n, ())
             if len(step) == 2:
                 flip_half(*step)

@@ -24,7 +24,8 @@ CHUNKS = ROW_TILES // CHUNK_TILES
 HALF_TILES = CHUNK_TILES // 2
 WORD_HALVES = 2
 POS, NEG = 0, 1
-PARTS = 2 * CHUNKS
+PARTS = 2 * CHUNKS + 1
+SECOND_HALF = 2 * CHUNKS
 TEMPERATURE = 0.07
 MASK_ROOT = 2.0**50
 FAR_BELOW = -1.0e30
@@ -32,14 +33,8 @@ FAR_BELOW = -1.0e30
 CHUNK_ORDER = [("anchor", c) for c in range(CHUNKS)] + [("pos", c) for c in range(CHUNKS)]
 
 
-STEP_BANKS = 6
-EARLY_STEPS = [(2, 1), (1,)]
-LATER_STEPS = [(2,)] + [step for k in range(3, 2 * CHUNKS - 1) for step in ((k, 0), (k, 1), (k,))]
-PREPARATION = dict(
-    list(enumerate(EARLY_STEPS))
-    + [(STEP_BANKS * (i + 1), step) for i, step in enumerate(LATER_STEPS)]
-    + [(106, (2 * CHUNKS - 1,))]
-)
+FLIP_EVERY = 4
+QUANTISE_LEAD = 4
 
 WARM_UP = 7
 
@@ -49,9 +44,18 @@ FLOPS = 2 * 2 * ROWS * ROWS * FEATURES
 def banks_opened_by(stage):
     name, chunk = CHUNK_ORDER[stage]
     if name == "pos":
-        return [(r, POS, chunk) for r in range(ROW_TILES)]
+        return [(r, POS, chunk * CHUNK_TILES, CHUNK_TILES) for r in range(ROW_TILES)]
+    if chunk == 0:
+        return [
+            (0, NEG, 0, HALF_TILES),
+            (1, NEG, 0, HALF_TILES),
+            (0, NEG, HALF_TILES, HALF_TILES),
+            (1, NEG, HALF_TILES, HALF_TILES),
+            (2, NEG, 0, CHUNK_TILES),
+            (3, NEG, 0, CHUNK_TILES),
+        ]
     return [
-        (r, NEG, c)
+        (r, NEG, c * CHUNK_TILES, CHUNK_TILES)
         for r in range((chunk + 1) * CHUNK_TILES)
         for c in range(chunk + 1)
         if r // CHUNK_TILES == chunk or c == chunk
@@ -63,7 +67,7 @@ def tile_crossgenderinfonceloss_pa_kernel(tc, anchor, pos, out):
     with ExitStack() as stack:
         stack.enter_context(tc.manual_schedule())
         keep = stack.enter_context(tc.tile_pool(name="keep", bufs=1))
-        stage_pool = stack.enter_context(tc.tile_pool(name="stage", bufs=3))
+        stage_pool = stack.enter_context(tc.tile_pool(name="stage", bufs=7))
         unread = stack.enter_context(tc.tile_pool(name="unread", bufs=4))
         psum = stack.enter_context(tc.psum_pool(name="psum", bufs=PSUM_BANKS))
 
@@ -135,6 +139,8 @@ def tile_crossgenderinfonceloss_pa_kernel(tc, anchor, pos, out):
         total = keep.tile([P, ROW_TILES * PARTS], F32)
         weight = keep.tile([P, 2, ROW_TILES, PARTS], F32)
         nc.vector.memset(weight[:], FAR_BELOW)
+        nc.vector.memset(shift[:], 2.0**100)
+        nc.vector.memset(total[:], 0.0)
 
         grouped = {CHUNK_ORDER[-1]: gathered}
 
@@ -156,18 +162,18 @@ def tile_crossgenderinfonceloss_pa_kernel(tc, anchor, pos, out):
             target = grouped[name, chunk][:].bitcast(F32)[:, rows, :]
             target = target.rearrange("p (t r) u -> p t r u", t=HALF_TILES)
             source = flipped[:].rearrange("p t u r -> p t r u")
-            if half == 0 or place in (1, 2):
+            if half == 0 or CHUNK_ORDER[place][0] == "anchor":
                 nc.scalar.copy(out=target, in_=source)
             else:
                 nc.vector.tensor_copy(out=target, in_=source)
 
-        def quantise(place):
+        def quantise(place, first=0, tiles=CHUNK_TILES):
             name, chunk = CHUNK_ORDER[place]
-            cols = slice(chunk * BANK, (chunk + 1) * BANK)
+            cols = slice((chunk * CHUNK_TILES + first) * P, (chunk * CHUNK_TILES + first + tiles) * P)
             nc.vector.quantize_mx(
                 out=codes[name][:, cols].bitcast(FP8X4),
                 scales=scales[name][:, cols],
-                in_=grouped[name, chunk][:].rearrange("p w j -> p (w j)"),
+                in_=grouped[name, chunk][:, first * P : (first + tiles) * P, :].rearrange("p w j -> p (w j)"),
             )
 
         def product(acc, r, name, cols, start, stop):
@@ -182,11 +188,12 @@ def tile_crossgenderinfonceloss_pa_kernel(tc, anchor, pos, out):
                 stop=stop,
             )
 
-        def open_bank(r, x, chunk):
-            acc = psum.tile([P, BANK], F32, tag="bank")
-            if x == NEG and chunk == r // CHUNK_TILES:
-                for t in range(CHUNK_TILES):
-                    other = chunk * CHUNK_TILES + t
+        def open_bank(r, x, first, tiles):
+            bank = psum.tile([P, BANK], F32, tag="bank")
+            acc = bank[:, 0 : tiles * P]
+            if x == NEG and first <= r < first + tiles:
+                for t in range(tiles):
+                    other = first + t
                     part = acc[:, t * P : (t + 1) * P]
                     product(part, r, "anchor", slice(other * P, (other + 1) * P), True, other != r)
                     if other == r:
@@ -201,9 +208,12 @@ def tile_crossgenderinfonceloss_pa_kernel(tc, anchor, pos, out):
                         )
             else:
                 name = "pos" if x == POS else "anchor"
-                product(acc[:], r, name, slice(chunk * BANK, (chunk + 1) * BANK), True, True)
-            col = slice(r * PARTS + x * CHUNKS + chunk, r * PARTS + x * CHUNKS + chunk + 1)
-            nc.vector.tensor_reduce(out=top[:, col], in_=acc[:], axis=AXIS_X, op=ALU.max)
+                product(acc, r, name, slice(first * P, (first + tiles) * P), True, True)
+            place = x * CHUNKS + first // CHUNK_TILES
+            if first % CHUNK_TILES:
+                place = SECOND_HALF
+            col = slice(r * PARTS + place, r * PARTS + place + 1)
+            nc.vector.tensor_reduce(out=top[:, col], in_=acc, axis=AXIS_X, op=ALU.max)
             nc.gpsimd.tensor_scalar(
                 out=shift[:, col],
                 in0=top[:, col],
@@ -217,36 +227,43 @@ def tile_crossgenderinfonceloss_pa_kernel(tc, anchor, pos, out):
         def close_bank(acc, col):
             exps = unread.tile([P, BANK], BF16)
             nc.scalar.activation(
-                out=exps[:],
-                in_=acc[:],
+                out=exps[:, 0 : acc.shape[1]],
+                in_=acc,
                 func=ACT.Exp,
                 bias=shift[:, col],
                 scale=1.0 / TEMPERATURE,
                 accum_out=total[:, col],
             )
 
-        flip_half(0, 0)
-        flip_half(0, 1)
-        quantise(0)
-        flip_half(1, 0)
-        flip_half(1, 1)
-        flip_half(2, 0)
-        still_open = None
         banks = []
+        steps = {}
         for place in range(len(CHUNK_ORDER)):
+            if place > 1:
+                steps.setdefault(len(banks) - QUANTISE_LEAD, []).append((quantise, (place,)))
             banks.extend(banks_opened_by(place))
-        for n, (r, x, chunk) in enumerate(banks):
-            newest = open_bank(r, x, chunk)
+        later_halves = [(place, half) for place in range(2, len(CHUNK_ORDER) - 1) for half in range(2)]
+        for i, later_half in enumerate(later_halves):
+            steps.setdefault(1 + FLIP_EVERY * i, []).append((flip_half, later_half))
+
+        flip_half(0, 0)
+        quantise(0, 0, HALF_TILES)
+        flip_half(0, 1)
+        flip_half(1, 0)
+        still_open = None
+        for n, (r, x, first, tiles) in enumerate(banks):
+            newest = open_bank(r, x, first, tiles)
             if still_open is not None:
                 close_bank(*still_open)
             still_open = newest
+            if n == 1:
+                quantise(0, HALF_TILES, HALF_TILES)
+                flip_half(1, 1)
+            if n == 4:
+                quantise(1)
             if n == 8:
                 gather(nc.scalar, CHUNK_TILES - 1)
-            step = PREPARATION.get(n, ())
-            if len(step) == 2:
-                flip_half(*step)
-            elif len(step) == 1:
-                quantise(*step)
+            for step, arguments in steps.get(n, []):
+                step(*arguments)
 
         shift_r = shift[:].rearrange("p (r b) -> p r b", b=PARTS)
         total_r = total[:].rearrange("p (r b) -> p r b", b=PARTS)

@@ -284,8 +284,8 @@ def tile_crossgenderinfonceloss_pa_kernel(tc, anchor, pos, out):
         )
         gap = keep.tile([P, ROW_TILES], F32)
         nc.vector.tensor_tensor(out=gap[:], in0=low[:, 1, :], in1=low[:, 0, :], op=ALU.subtract)
-        nc.scalar.activation(out=weight[:], in_=weight[:], func=ACT.Exp)
         close_bank(*still_open)
+        nc.scalar.activation(out=weight[:], in_=weight[:], func=ACT.Exp)
         nc.scalar.activation(out=zero_again[:], in_=one[:], func=ACT.Ln)
         nc.vector.tensor_tensor(
             out=weight[:],

@@ -162,7 +162,7 @@ def tile_crossgenderinfonceloss_pa_kernel(tc, anchor, pos, out):
             target = grouped[name, chunk][:].bitcast(F32)[:, rows, :]
             target = target.rearrange("p (t r) u -> p t r u", t=HALF_TILES)
             source = flipped[:].rearrange("p t u r -> p t r u")
-            if half == 0 or CHUNK_ORDER[place][0] == "anchor":
+            if half == 0 or place < 3:
                 nc.scalar.copy(out=target, in_=source)
             else:
                 nc.vector.tensor_copy(out=target, in_=source)

from contextlib import ExitStack

import concourse.mybir as mybir
from concourse.masks import make_identity

F32 = mybir.dt.float32
BF16 = mybir.dt.bfloat16
U32 = mybir.dt.uint32
U8 = mybir.dt.uint8
FP8X4 = mybir.dt.float8_e4m3fn_x4
ALU = mybir.AluOpType
ACT = mybir.ActivationFunctionType
AXIS_X = mybir.AxisListType.X

P = 128
PACK = 4
ROWS = 2048
FEATURES = 512
ROW_TILES = ROWS // P
BANK = 512
PSUM_BANKS = 8
CHUNK_TILES = BANK // P
CHUNKS = ROW_TILES // CHUNK_TILES
HALF_TILES = CHUNK_TILES // 2
WORD_HALVES = 2
POS, NEG = 0, 1
PARTS = 2 * CHUNKS + 1
SECOND_HALF = 2 * CHUNKS
TEMPERATURE = 0.07
MASK_ROOT = 2.0**50
FAR_BELOW = -1.0e30

CHUNK_ORDER = [("anchor", c) for c in range(CHUNKS)] + [("pos", c) for c in range(CHUNKS)]


FLIP_EVERY = 4
QUANTISE_LEAD = 4

WARM_UP = 7

FLOPS = 2 * 2 * ROWS * ROWS * FEATURES


def banks_opened_by(stage):
    name, chunk = CHUNK_ORDER[stage]
    if name == "pos":
        return [(r, POS, chunk * CHUNK_TILES, CHUNK_TILES) for r in range(ROW_TILES)]
    if chunk == 0:
        return [
            (0, NEG, 0, HALF_TILES),
            (1, NEG, 0, HALF_TILES),
            (0, NEG, HALF_TILES, HALF_TILES),
            (1, NEG, HALF_TILES, HALF_TILES),
            (2, NEG, 0, CHUNK_TILES),
            (3, NEG, 0, CHUNK_TILES),
        ]
    return [
        (r, NEG, c * CHUNK_TILES, CHUNK_TILES)
        for r in range((chunk + 1) * CHUNK_TILES)
        for c in range(chunk + 1)
        if r // CHUNK_TILES == chunk or c == chunk
    ]


def tile_crossgenderinfonceloss_pa_kernel(tc, anchor, pos, out):
    nc = tc.nc
    with ExitStack() as stack:
        stack.enter_context(tc.manual_schedule())
        keep = stack.enter_context(tc.tile_pool(name="keep", bufs=1))
        stage_pool = stack.enter_context(tc.tile_pool(name="stage", bufs=7))
        unread = stack.enter_context(tc.tile_pool(name="unread", bufs=4))
        psum = stack.enter_context(tc.psum_pool(name="psum", bufs=PSUM_BANKS))

        sources = {"anchor": anchor, "pos": pos}
        raw = {}
        for name in ("anchor", "pos"):
            raw[name] = keep.tile([P, ROW_TILES, FEATURES], BF16, name="raw_" + name)
        loads = [(name, chunk * CHUNK_TILES, HALF_TILES) for name, chunk in CHUNK_ORDER]
        loads = [(name, first + half * tiles, tiles) for name, first, tiles in loads for half in range(2)]
        loads = [("anchor", 0, 1), ("anchor", 1, 1)] + loads[1:]
        for name, first, tiles in loads[: len(loads) - 2]:
            nc.sync.dma_start(
                out=raw[name][:, first : first + tiles, :],
                in_=sources[name].rearrange("(p r) k -> p r k", r=ROW_TILES)[:, first : first + tiles, :],
            )

        gathered = keep.tile([P, BANK, PACK], BF16, align_bytes=64)

        def gather(queue, t):
            name, chunk = CHUNK_ORDER[-1]
            queue.dma_start(
                out=gathered[:, t * P : (t + 1) * P, :],
                in_=sources[name].rearrange("(w r) (q j) -> q r w j", r=ROW_TILES, j=PACK)[
                    :, chunk * CHUNK_TILES + t
                ],
            )

        for t in range(CHUNK_TILES - 1):
            gather(nc.sync, t)

        nothing = keep.tile([P, 2 * P], BF16)
        nc.vector.memset(nothing[:], 0.0)
        nowhere = psum.tile([P, BANK], F32, tag="bank")
        for i in range(WARM_UP):
            nc.tensor.matmul(nowhere[:, 0 : 2 * P], lhsT=nothing[:, 0:P], rhs=nothing[:], start=True, stop=True)

        identity = keep.tile([P, P], F32)
        make_identity(nc, identity[:])
        zero = keep.tile([P, 1], F32)
        nc.vector.memset(zero[:], 0.0)
        one = keep.tile([P, 1], F32)
        nc.scalar.activation(out=one[:], in_=zero[:], func=ACT.Exp)
        zero_again = keep.tile([P, 1], F32)

        mask_values = keep.tile([P, 2, P, PACK], BF16, align_bytes=64)
        spread_identity = identity[:].unsqueeze(2).to_broadcast([P, P, PACK])
        nc.vector.tensor_scalar(
            out=mask_values[:, 0], in0=spread_identity, scalar1=MASK_ROOT, scalar2=None, op0=ALU.mult
        )
        nc.vector.tensor_scalar(
            out=mask_values[:, 1], in0=spread_identity, scalar1=-MASK_ROOT, scalar2=None, op0=ALU.mult
        )
        mask_codes = keep.tile([P, 2 * P], U32, align_bytes=64)
        mask_scales = keep.tile([P, 2 * P], U8, align_bytes=64)
        nc.vector.quantize_mx(
            out=mask_codes[:].bitcast(FP8X4),
            scales=mask_scales[:],
            in_=mask_values[:].rearrange("p s m j -> p (s m j)"),
        )

        codes = {}
        scales = {}
        for name in ("anchor", "pos"):
            codes[name] = keep.tile([P, ROWS], U32, name="codes_" + name, align_bytes=64)
            scales[name] = keep.tile([P, ROWS], U8, name="scales_" + name, align_bytes=64)

        top = keep.tile([P, ROW_TILES * PARTS], F32)
        shift = keep.tile([P, ROW_TILES * PARTS], F32)
        total = keep.tile([P, ROW_TILES * PARTS], F32)
        weight = keep.tile([P, 2, ROW_TILES, PARTS], F32)
        nc.vector.memset(weight[:], FAR_BELOW)
        nc.vector.memset(shift[:], 2.0**100)
        nc.vector.memset(total[:], 0.0)

        grouped = {CHUNK_ORDER[-1]: gathered}

        def flip_half(place, half):
            name, chunk = CHUNK_ORDER[place]
            if half == 0:
                grouped[name, chunk] = stage_pool.tile(
                    [P, BANK, PACK], BF16, name="grouped", align_bytes=64
                )
            words = raw[name][:].bitcast(F32)
            flipped = psum.tile([P, HALF_TILES, WORD_HALVES, P], F32, tag="bank")
            for t in range(HALF_TILES):
                r = chunk * CHUNK_TILES + half * HALF_TILES + t
                for u in range(WORD_HALVES):
                    nc.tensor.transpose(
                        flipped[:, t, u, :], words[:, r, u : WORD_HALVES * P : WORD_HALVES], identity[:]
                    )
            rows = slice(half * HALF_TILES * P, (half + 1) * HALF_TILES * P)
            target = grouped[name, chunk][:].bitcast(F32)[:, rows, :]
            target = target.rearrange("p (t r) u -> p t r u", t=HALF_TILES)
            source = flipped[:].rearrange("p t u r -> p t r u")
            if half == 0 or place < 3:
                nc.scalar.copy(out=target, in_=source)
            else:
                nc.vector.tensor_copy(out=target, in_=source)

        def quantise(place, first=0, tiles=CHUNK_TILES):
            name, chunk = CHUNK_ORDER[place]
            cols = slice((chunk * CHUNK_TILES + first) * P, (chunk * CHUNK_TILES + first + tiles) * P)
            nc.vector.quantize_mx(
                out=codes[name][:, cols].bitcast(FP8X4),
                scales=scales[name][:, cols],
                in_=grouped[name, chunk][:, first * P : (first + tiles) * P, :].rearrange("p w j -> p (w j)"),
            )

        def product(acc, r, name, cols, start, stop):
            rows = slice(r * P, (r + 1) * P)
            nc.tensor.matmul_mx(
                out=acc,
                lhsT=codes["anchor"][:, rows].bitcast(FP8X4),
                lhsT_scale=scales["anchor"][:, rows],
                rhs=codes[name][:, cols].bitcast(FP8X4),
                rhs_scale=scales[name][:, cols],
                start=start,
                stop=stop,
            )

        def open_bank(r, x, first, tiles):
            bank = psum.tile([P, BANK], F32, tag="bank")
            acc = bank[:, 0 : tiles * P]
            if x == NEG and first <= r < first + tiles:
                for t in range(tiles):
                    other = first + t
                    part = acc[:, t * P : (t + 1) * P]
                    product(part, r, "anchor", slice(other * P, (other + 1) * P), True, other != r)
                    if other == r:
                        nc.tensor.matmul_mx(
                            out=part,
                            lhsT=mask_codes[:, 0:P].bitcast(FP8X4),
                            lhsT_scale=mask_scales[:, 0:P],
                            rhs=mask_codes[:, P : 2 * P].bitcast(FP8X4),
                            rhs_scale=mask_scales[:, P : 2 * P],
                            start=False,
                            stop=True,
                        )
            else:
                name = "pos" if x == POS else "anchor"
                product(acc, r, name, slice(first * P, (first + tiles) * P), True, True)
            place = x * CHUNKS + first // CHUNK_TILES
            if first % CHUNK_TILES:
                place = SECOND_HALF
            col = slice(r * PARTS + place, r * PARTS + place + 1)
            nc.vector.tensor_reduce(out=top[:, col], in_=acc, axis=AXIS_X, op=ALU.max)
            nc.gpsimd.tensor_scalar(
                out=shift[:, col],
                in0=top[:, col],
                scalar1=-1.0 / TEMPERATURE,
                scalar2=0.0,
                op0=ALU.mult,
                op1=ALU.add,
            )
            return acc, col

        def close_bank(acc, col):
            exps = unread.tile([P, BANK], BF16)
            nc.scalar.activation(
                out=exps[:, 0 : acc.shape[1]],
                in_=acc,
                func=ACT.Exp,
                bias=shift[:, col],
                scale=1.0 / TEMPERATURE,
                accum_out=total[:, col],
            )

        banks = []
        steps = {}
        for place in range(len(CHUNK_ORDER)):
            if place > 1:
                steps.setdefault(len(banks) - QUANTISE_LEAD, []).append((quantise, (place,)))
            banks.extend(banks_opened_by(place))
        later_halves = [(place, half) for place in range(2, len(CHUNK_ORDER) - 1) for half in range(2)]
        for i, later_half in enumerate(later_halves):
            steps.setdefault(1 + FLIP_EVERY * i, []).append((flip_half, later_half))

        flip_half(0, 0)
        quantise(0, 0, HALF_TILES)
        flip_half(0, 1)
        flip_half(1, 0)
        still_open = None
        for n, (r, x, first, tiles) in enumerate(banks):
            newest = open_bank(r, x, first, tiles)
            if still_open is not None:
                close_bank(*still_open)
            still_open = newest
            if n == 1:
                quantise(0, HALF_TILES, HALF_TILES)
                flip_half(1, 1)
            if n == 4:
                quantise(1)
            if n == 8:
                gather(nc.scalar, CHUNK_TILES - 1)
            for step, arguments in steps.get(n, []):
                step(*arguments)

        shift_r = shift[:].rearrange("p (r b) -> p r b", b=PARTS)
        total_r = total[:].rearrange("p (r b) -> p r b", b=PARTS)
        low = keep.tile([P, 2, ROW_TILES], F32)
        nc.vector.tensor_reduce(out=low[:, 0, :], in_=shift_r[:, :, 0:CHUNKS], axis=AXIS_X, op=ALU.min)
        nc.vector.tensor_reduce(out=low[:, 1, :], in_=shift_r, axis=AXIS_X, op=ALU.min)
        nc.vector.tensor_tensor(
            out=weight[:, 0, :, 0:CHUNKS],
            in0=low[:, 0, :].unsqueeze(2).to_broadcast([P, ROW_TILES, CHUNKS]),
            in1=shift_r[:, :, 0:CHUNKS],
            op=ALU.subtract,
        )
        nc.vector.tensor_tensor(
            out=weight[:, 1],
            in0=low[:, 1, :].unsqueeze(2).to_broadcast([P, ROW_TILES, PARTS]),
            in1=shift_r,
            op=ALU.subtract,
        )
        gap = keep.tile([P, ROW_TILES], F32)
        nc.vector.tensor_tensor(out=gap[:], in0=low[:, 1, :], in1=low[:, 0, :], op=ALU.subtract)
        close_bank(*still_open)
        nc.scalar.activation(out=weight[:], in_=weight[:], func=ACT.Exp)
        nc.scalar.activation(out=zero_again[:], in_=one[:], func=ACT.Ln)
        nc.vector.tensor_tensor(
            out=weight[:],
            in0=weight[:],
            in1=total_r.unsqueeze(1).to_broadcast([P, 2, ROW_TILES, PARTS]),
            op=ALU.mult,
        )
        sums = keep.tile([P, 2, ROW_TILES], F32)
        nc.vector.tensor_reduce(out=sums[:], in_=weight[:], axis=AXIS_X, op=ALU.add)
        ratio = keep.tile([P, ROW_TILES], F32)
        nc.vector.reciprocal(out=ratio[:], in_=sums[:, 1, :])
        nc.vector.tensor_tensor(out=ratio[:], in0=ratio[:], in1=sums[:, 0, :], op=ALU.mult)
        result = keep.tile([P, ROW_TILES], F32)
        nc.scalar.activation(out=result[:], in_=ratio[:], func=ACT.Ln)
        nc.vector.tensor_tensor(out=result[:], in0=result[:], in1=gap[:], op=ALU.add)
        nc.sync.dma_start(out=out.rearrange("(p r) -> p r", r=ROW_TILES), in_=result[:])
